import numpy as np
import ml_dtypes


def mxq(x, axis, fmt="e4m3"):
    dtype, down = {"e4m3": (ml_dtypes.float8_e4m3fn, 7), "e5m2": (ml_dtypes.float8_e5m2, 14)}[fmt]
    v = np.moveaxis(np.asarray(x, np.float32).astype(ml_dtypes.bfloat16).astype(np.float64), axis, -1)
    blocks = v.reshape(v.shape[:-1] + (-1, 32))
    amax = np.abs(blocks).max(-1, keepdims=True)
    byte = np.maximum(np.where(amax > 0, np.frexp(amax)[1] - 1 + 127, 0) - down, 1)
    scale = np.exp2(byte - 127.0)
    codes = (blocks / scale).astype(np.float32).astype(dtype).astype(np.float64)
    return np.moveaxis((codes * scale).reshape(v.shape), -1, axis)


WIDE = False


def mx_kscale(k):
    if not WIDE:
        return np.ones(k)
    levels = np.array([10, -10, 5, -5, 0])
    if k % 512:
        return np.exp2(np.random.permutation(np.resize(levels, k // 32))).repeat(32)
    a = np.empty((k // 512, 16))
    for p in range(k // 512):
        a[p, :8] = np.random.permutation(np.resize(levels, 8))
        for g in range(8):
            far = levels[np.abs(levels - a[p, g]) >= 10]
            a[p, g + 8] = far[np.random.randint(len(far))]
    return np.exp2(a.ravel()).repeat(32)


BF16 = ml_dtypes.bfloat16


def bf(x):
    return np.asarray(x, np.float32).astype(BF16)


def f64(x):
    return np.asarray(x).astype(np.float64)


B, CH, CQ, CV, H, W = 1, 1024, 128, 512, 32, 64
EPS = 1e-5
POOL = 2
HW = H * W
HW4 = HW // (POOL * POOL)
A = 1.5 / CQ ** 0.25


def bn(y, s, b, m, v):
    inv = f64(s) / np.sqrt(f64(v) + EPS)
    return y * inv[None, :, None] + (f64(b) - f64(m) * inv)[None, :, None]


def maxpool(y):
    c = y.shape[1]
    return y.reshape(B, c, H // POOL, POOL, W // POOL, POOL).max(axis=(3, 5)).reshape(B, c, HW4)


def vec(c, z):
    return bf(z * np.random.standard_normal(c))


def pos(c):
    return bf(0.5 + np.random.random(c))


def setup_inputs():
    s = mx_kscale(CH)
    return {'memory': bf(np.random.standard_normal((B, CH, H, W)) * s[None, :, None, None]),
            'wq': bf(np.random.standard_normal((CQ, CH)) * A / np.sqrt(CH) / s), 'bq': vec(CQ, 0.1),
            'bnq_s': pos(CQ), 'bnq_b': vec(CQ, 0.1), 'bnq_m': vec(CQ, 0.1), 'bnq_v': pos(CQ),
            'wk': bf(np.random.standard_normal((CQ, CH)) * A / np.sqrt(CH) / s), 'bk': vec(CQ, 0.1),
            'bnk_s': pos(CQ), 'bnk_b': vec(CQ, 0.1), 'bnk_m': vec(CQ, 0.1), 'bnk_v': pos(CQ),
            'wv': bf(np.random.standard_normal((CV, CH)) / np.sqrt(CH) / s), 'bv': vec(CV, 0.3),
            'bnv_s': pos(CV), 'bnv_b': vec(CV, 0.3), 'bnv_m': vec(CV, 0.3), 'bnv_v': pos(CV)}


def reference(memory, wq, bq, bnq_s, bnq_b, bnq_m, bnq_v, wk, bk, bnk_s, bnk_b, bnk_m, bnk_v, wv, bv, bnv_s, bnv_b, bnv_m, bnv_v):
    mq = mxq(f64(memory).reshape(B, CH, HW), 1, 'e4m3')
    yq = (mxq(f64(wq), 1, 'e4m3') @ mq) + f64(bq)[None, :, None]
    yk = (mxq(f64(wk), 1, 'e4m3') @ mq) + f64(bk)[None, :, None]
    yv = (mxq(f64(wv), 1, 'e4m3') @ mq) + f64(bv)[None, :, None]
    q = bn(yq, bnq_s, bnq_b, bnq_m, bnq_v).transpose(0, 2, 1)
    k = maxpool(bn(yk, bnk_s, bnk_b, bnk_m, bnk_v))
    v = maxpool(bn(yv, bnv_s, bnv_b, bnv_m, bnv_v)).transpose(0, 2, 1)
    return q, k, v

@@ -1,0 +1,250 @@
+from contextlib import ExitStack
+
+import concourse.masks as masks
+import concourse.mybir as mybir
+
+F32 = mybir.dt.float32
+BF16 = mybir.dt.bfloat16
+U32 = mybir.dt.uint32
+U8 = mybir.dt.uint8
+FP8X4 = mybir.dt.float8_e4m3fn_x4
+IDENTITY = mybir.ActivationFunctionType.Identity
+
+P = 128
+PACK = 4
+K_PASS = P * PACK
+CH = 1024
+PASSES = CH // K_PASS
+WIDTH = 64
+POSITIONS = 32 * WIDTH
+CHUNK = 512
+CHUNKS = POSITIONS // CHUNK
+POOLED = CHUNK // 4
+V_BLOCKS = 4
+Q_BLOCK = 4
+K_BLOCK = 5
+BLOCKS = 6
+POOL_BLOCKS = V_BLOCKS + 1
+KINDS = 5
+EPS = 1e-5
+
+FLOPS = 2 * BLOCKS * P * CH * POSITIONS
+
+
+def tile_selfattention_pa_kernel(
+    tc,
+    memory,
+    wq, bq, bnq_s, bnq_b, bnq_m, bnq_v,
+    wk, bk, bnk_s, bnk_b, bnk_m, bnk_v,
+    wv, bv, bnv_s, bnv_b, bnv_m, bnv_v,
+    out_0, out_1, out_2,
+):
+    nc = tc.nc
+    with ExitStack() as ctx:
+        keep = ctx.enter_context(tc.tile_pool(name="keep", bufs=1))
+        resident = ctx.enter_context(tc.tile_pool(name="resident", bufs=CHUNKS))
+        stream = ctx.enter_context(tc.tile_pool(name="stream", bufs=2))
+        psum = ctx.enter_context(tc.psum_pool(name="psum", bufs=8))
+        ctx.enter_context(tc.manual_schedule())
+
+
+        vec_rows = keep.tile([P, P], BF16)
+        nc.gpsimd.memset(vec_rows[:], 0.0)
+        identity = keep.tile([P, P], F32)
+        nc.vector.memset(identity[:], 0.0)
+        masks.make_identity(nc, identity[:], nomemset=True)
+        warm = keep.tile([P, 1], F32)
+        nc.vector.memset(warm[:], 1.0)
+        nc.scalar.sqrt(out=warm[:], in_=warm[:])
+        q_vectors = (bq, bnq_s, bnq_b, bnq_m, bnq_v)
+        k_vectors = (bk, bnk_s, bnk_b, bnk_m, bnk_v)
+        v_vectors = (bv, bnv_s, bnv_b, bnv_m, bnv_v)
+
+        def load_vectors(vectors, first_block, blocks):
+            for kind, vector in enumerate(vectors):
+                row = BLOCKS * kind + first_block
+                nc.sync.dma_start(
+                    out=vec_rows[row : row + blocks, :],
+                    in_=vector.rearrange("(b c) -> b c", c=P),
+                )
+
+        mem_rows = memory.rearrange("b (g p t) h w -> p (b g) t (h w)", p=P, t=PACK)
+
+        def load_chunk(c):
+            raw = resident.tile([P, PASSES, PACK, CHUNK], BF16, name="mem_raw")
+            for g in range(PASSES):
+                nc.sync.dma_start(
+                    out=raw[:, g, :, :],
+                    in_=mem_rows[:, g, :, c * CHUNK : (c + 1) * CHUNK],
+                )
+            return raw
+
+        w_raw = keep.tile([P, BLOCKS, CH], BF16)
+        wv_blocks = wv.rearrange("(b r) k -> r b k", r=P)
+
+        load_vectors(v_vectors, 0, V_BLOCKS)
+        mem_raw = [load_chunk(0)]
+        nc.sync.dma_start(out=w_raw[:, 0:2, :], in_=wv_blocks[:, 0:2, :])
+        load_vectors(q_vectors, Q_BLOCK, 1)
+        nc.sync.dma_start(out=w_raw[:, 2:4, :], in_=wv_blocks[:, 2:4, :])
+        nc.sync.dma_start(out=w_raw[:, Q_BLOCK, :], in_=wq)
+        nc.sync.dma_start(out=w_raw[:, K_BLOCK, :], in_=wk)
+        load_vectors(k_vectors, K_BLOCK, 1)
+        for c in range(1, CHUNKS):
+            mem_raw.append(load_chunk(c))
+
+        def quantise_chunk(c):
+            grouped = stream.tile([P, PASSES, CHUNK, PACK], BF16, align_bytes=64, name="grouped")
+            for g in range(PASSES):
+                nc.vector.tensor_copy(
+                    out=grouped[:, g, :, :].rearrange("p (c i) t -> p c t i", i=4),
+                    in_=mem_raw[c][:, g, :, :].rearrange("p t (c i) -> p c t i", i=4),
+                )
+            codes = stream.tile([P, PASSES, CHUNK], U32, align_bytes=64, name="codes")
+            scales = stream.tile([P, PASSES, CHUNK], U8, align_bytes=64, name="scales")
+            for g in range(PASSES):
+                nc.vector.quantize_mx(
+                    out=codes[:, g, :].bitcast(FP8X4),
+                    scales=scales[:, g, :],
+                    in_=grouped[:, g, :, :].rearrange("p n t -> p (n t)"),
+                )
+            return codes, scales
+
+        w_grouped = keep.tile([P, BLOCKS, CH], BF16, align_bytes=64)
+        w_codes = keep.tile([P, BLOCKS, PASSES * P], U32, align_bytes=64)
+        w_scales = keep.tile([P, BLOCKS, PASSES * P], U8, align_bytes=64)
+
+        def transpose_weights(m):
+            words = w_raw[:, m, :].bitcast(F32)
+            bank = psum.tile([P, CHUNK], F32, name="bank")
+            for g in range(PASSES):
+                for u in range(2):
+                    j = 2 * g + u
+                    nc.tensor.transpose(
+                        bank[:, j * P : (j + 1) * P],
+                        words[:, 2 * P * g + u : 2 * P * (g + 1) : 2],
+                        identity[:],
+                    )
+            nc.scalar.copy(
+                out=w_grouped[:, m, :].bitcast(F32).rearrange("p (g r u) -> p g r u", g=PASSES, u=2),
+                in_=bank[:].rearrange("p (g u r) -> p g r u", g=PASSES, u=2),
+            )
+
+        def quantise_weights(first, blocks):
+            nc.vector.quantize_mx(
+                out=w_codes[:, first : first + blocks, :].rearrange("p m w -> p (m w)").bitcast(FP8X4),
+                scales=w_scales[:, first : first + blocks, :].rearrange("p m w -> p (m w)"),
+                in_=w_grouped[:, first : first + blocks, :].rearrange("p m k -> p (m k)"),
+            )
+
+        inv = keep.tile([P, BLOCKS], F32)
+        shift = keep.tile([P, BLOCKS], F32)
+
+        columns = keep.tile([P, KINDS, BLOCKS], F32)
+        bias, gain, beta, mean, var = [columns[:, kind, :] for kind in range(KINDS)]
+        std = keep.tile([P, BLOCKS], F32)
+
+        vec_f32 = keep.tile([P, P], F32)
+
+        def widen_vectors():
+            nc.vector.tensor_copy(out=vec_f32[:], in_=vec_rows[:])
+
+        def turn_vectors():
+            bank = psum.tile([P, CHUNK], F32, name="bank")
+            nc.tensor.transpose(bank[:, 0:P], vec_f32[:], identity[:])
+            nc.vector.tensor_copy(
+                out=columns[:].rearrange("p k b -> p (k b)"), in_=bank[:, 0 : KINDS * BLOCKS]
+            )
+            nc.vector.tensor_scalar_add(out=std[:], in0=var, scalar1=EPS)
+            nc.scalar.sqrt(out=std[:], in_=std[:])
+            nc.vector.tensor_sub(out=shift[:], in0=bias, in1=mean)
+
+        def fold_batch_norms():
+            nc.vector.reciprocal(out=inv[:], in_=std[:])
+            nc.vector.tensor_mul(out=inv[:], in0=inv[:], in1=gain)
+            nc.vector.tensor_mul(out=shift[:], in0=shift[:], in1=inv[:])
+            nc.vector.tensor_add(out=shift[:], in0=shift[:], in1=beta)
+
+        def project(m, codes, scales):
+            bank = psum.tile([P, CHUNK], F32, name="bank")
+            for g in range(PASSES):
+                nc.tensor.matmul_mx(
+                    out=bank[:],
+                    lhsT=w_codes[:, m, g * P : (g + 1) * P].bitcast(FP8X4),
+                    lhsT_scale=w_scales[:, m, g * P : (g + 1) * P],
+                    rhs=codes[:, g, :].bitcast(FP8X4),
+                    rhs_scale=scales[:, g, :],
+                    start=(g == 0),
+                    stop=(g == PASSES - 1),
+                )
+            return bank
+
+        def convolve_chunk(codes, scales):
+            z = stream.tile([P, POOL_BLOCKS, CHUNK], F32, name="z", bufs=3)
+            zq = stream.tile([P, 4, P], F32, name="zq")
+            for m in range(BLOCKS):
+                bank = project(m, codes, scales)
+                if m == Q_BLOCK:
+                    source, target = bank[:].rearrange("p (j s) -> p s j", s=4), zq[:]
+                else:
+                    source, target = bank[:], z[:, min(m, V_BLOCKS), :]
+                nc.scalar.activation(
+                    out=target, in_=source,
+                    func=IDENTITY, bias=shift[:, m : m + 1], scale=inv[:, m : m + 1],
+                )
+            return zq, z
+
+
+        def finish_q(c, zq):
+            q_bank = psum.tile([P, CHUNK], F32, name="bank")
+            for s in range(4):
+                nc.tensor.transpose(q_bank[:, s * P : (s + 1) * P], zq[:, s, :], identity[:])
+            q_rows = resident.tile([P, CHUNK], F32, name="q_rows")
+            nc.scalar.copy(out=q_rows[:], in_=q_bank[:])
+            nc.sync.dma_start(
+                out=out_0[0, c * CHUNK : (c + 1) * CHUNK, :].rearrange("(j s) ch -> j (s ch)", s=4),
+                in_=q_rows[:],
+            )
+
+        def finish_kv(c, z):
+            row_pairs = z[:].rearrange("p b (a d w) -> p (b a) d w", d=2, w=WIDTH)
+            row_max = stream.tile([P, POOL_BLOCKS * CHUNK // (2 * WIDTH), WIDTH], F32, name="row_max")
+            nc.vector.tensor_max(out=row_max[:], in0=row_pairs[:, :, 0, :], in1=row_pairs[:, :, 1, :])
+            column_pairs = row_max[:].rearrange("p (b a) (x d) -> p b (a x) d", b=POOL_BLOCKS, d=2)
+            pooled = stream.tile([P, POOL_BLOCKS, POOLED], F32, name="pooled", bufs=3)
+            nc.vector.tensor_max(
+                out=pooled[:], in0=column_pairs[:, :, :, 0], in1=column_pairs[:, :, :, 1]
+            )
+            nc.sync.dma_start(
+                out=out_1[0, :, c * POOLED : (c + 1) * POOLED], in_=pooled[:, V_BLOCKS, :]
+            )
+
+            v_bank = psum.tile([P, CHUNK], F32, name="bank")
+            for b in range(V_BLOCKS):
+                nc.tensor.transpose(v_bank[:, b * P : (b + 1) * P], pooled[:, b, :], identity[:])
+            v_rows = resident.tile([P, CHUNK], F32, name="v_rows")
+            nc.scalar.copy(out=v_rows[:], in_=v_bank[:])
+            nc.sync.dma_start(out=out_2[0, c * POOLED : (c + 1) * POOLED, :], in_=v_rows[:])
+
+        quantised = [quantise_chunk(0)]
+        transpose_weights(0)
+        transpose_weights(1)
+        quantise_weights(0, 2)
+        widen_vectors()
+        transpose_weights(2)
+        transpose_weights(3)
+        transpose_weights(Q_BLOCK)
+        turn_vectors()
+        quantise_weights(2, 2)
+        transpose_weights(K_BLOCK)
+        fold_batch_norms()
+        quantise_weights(Q_BLOCK, 2)
+        results = []
+        for c in range(CHUNKS + 2):
+            if c < CHUNKS:
+                if c > 0:
+                    quantised.append(quantise_chunk(c))
+                results.append(convolve_chunk(*quantised[c]))
+                finish_q(c, results[c][0])
+            if c >= 2:
+                finish_kv(c - 2, results[c - 2][1])

@@ -9,6 +9,7 @@ U32 = mybir.dt.uint32
 U8 = mybir.dt.uint8
 FP8X4 = mybir.dt.float8_e4m3fn_x4
 IDENTITY = mybir.ActivationFunctionType.Identity
+SQRT = mybir.ActivationFunctionType.Sqrt
 
 P = 128
 PACK = 4
@@ -27,6 +28,7 @@ BLOCKS = 6
 POOL_BLOCKS = V_BLOCKS + 1
 KINDS = 5
 EPS = 1e-5
+SCALAR_COLUMNS = {(0, 0): 160}
 
 FLOPS = 2 * BLOCKS * P * CH * POSITIONS
 
@@ -42,73 +44,99 @@ def tile_selfattention_pa_kernel(
     nc = tc.nc
     with ExitStack() as ctx:
         keep = ctx.enter_context(tc.tile_pool(name="keep", bufs=1))
-        resident = ctx.enter_context(tc.tile_pool(name="resident", bufs=CHUNKS))
+        per_chunk = ctx.enter_context(tc.tile_pool(name="per_chunk", bufs=CHUNKS))
         stream = ctx.enter_context(tc.tile_pool(name="stream", bufs=2))
         psum = ctx.enter_context(tc.psum_pool(name="psum", bufs=8))
         ctx.enter_context(tc.manual_schedule())
 
-
-        vec_rows = keep.tile([P, P], BF16)
-        nc.gpsimd.memset(vec_rows[:], 0.0)
-        identity = keep.tile([P, P], F32)
-        nc.vector.memset(identity[:], 0.0)
-        masks.make_identity(nc, identity[:], nomemset=True)
+        v_vec_rows = keep.tile([P, P], BF16)
+        nc.gpsimd.memset(v_vec_rows[:], 0.0)
+        qk_vec_rows = keep.tile([P, P], BF16)
+        nc.gpsimd.memset(qk_vec_rows[:], 0.0)
         warm = keep.tile([P, 1], F32)
         nc.vector.memset(warm[:], 1.0)
         nc.scalar.sqrt(out=warm[:], in_=warm[:])
+        identity = keep.tile([P, P], F32)
+        nc.vector.memset(identity[:], 0.0)
+        masks.make_identity(nc, identity[:], nomemset=True)
         q_vectors = (bq, bnq_s, bnq_b, bnq_m, bnq_v)
         k_vectors = (bk, bnk_s, bnk_b, bnk_m, bnk_v)
         v_vectors = (bv, bnv_s, bnv_b, bnv_m, bnv_v)
 
-        def load_vectors(vectors, first_block, blocks):
+        def load_vectors(vec_rows, vectors, blocks, first, count):
             for kind, vector in enumerate(vectors):
-                row = BLOCKS * kind + first_block
+                row = blocks * kind + first
                 nc.sync.dma_start(
-                    out=vec_rows[row : row + blocks, :],
+                    out=vec_rows[row : row + count, :],
                     in_=vector.rearrange("(b c) -> b c", c=P),
                 )
 
         mem_rows = memory.rearrange("b (g p t) h w -> p (b g) t (h w)", p=P, t=PACK)
+        mem_raw = [per_chunk.tile([P, PASSES, PACK, CHUNK], BF16, name="mem_raw") for c in range(CHUNKS)]
 
-        def load_chunk(c):
-            raw = resident.tile([P, PASSES, PACK, CHUNK], BF16, name="mem_raw")
-            for g in range(PASSES):
-                nc.sync.dma_start(
-                    out=raw[:, g, :, :],
-                    in_=mem_rows[:, g, :, c * CHUNK : (c + 1) * CHUNK],
-                )
-            return raw
+        def load_memory(c, g):
+            nc.sync.dma_start(
+                out=mem_raw[c][:, g, :, :], in_=mem_rows[:, g, :, c * CHUNK : (c + 1) * CHUNK]
+            )
 
         w_raw = keep.tile([P, BLOCKS, CH], BF16)
         wv_blocks = wv.rearrange("(b r) k -> r b k", r=P)
 
-        load_vectors(v_vectors, 0, V_BLOCKS)
-        mem_raw = [load_chunk(0)]
-        nc.sync.dma_start(out=w_raw[:, 0:2, :], in_=wv_blocks[:, 0:2, :])
-        load_vectors(q_vectors, Q_BLOCK, 1)
-        nc.sync.dma_start(out=w_raw[:, 2:4, :], in_=wv_blocks[:, 2:4, :])
+        def load_v_weights(first, blocks):
+            nc.sync.dma_start(
+                out=w_raw[:, first : first + blocks, :], in_=wv_blocks[:, first : first + blocks, :]
+            )
+
+        load_memory(0, 0)
+        load_v_weights(0, 1)
+        load_memory(0, 1)
+        load_vectors(v_vec_rows, v_vectors, V_BLOCKS, 0, V_BLOCKS)
+        load_v_weights(1, 1)
+        load_v_weights(2, 2)
+        load_memory(1, 0)
+        load_vectors(qk_vec_rows, q_vectors, 2, 0, 1)
+        load_memory(1, 1)
         nc.sync.dma_start(out=w_raw[:, Q_BLOCK, :], in_=wq)
         nc.sync.dma_start(out=w_raw[:, K_BLOCK, :], in_=wk)
-        load_vectors(k_vectors, K_BLOCK, 1)
-        for c in range(1, CHUNKS):
-            mem_raw.append(load_chunk(c))
+        load_memory(2, 0)
+        load_memory(2, 1)
+        load_vectors(qk_vec_rows, k_vectors, 2, 1, 1)
+        load_memory(3, 0)
+        load_memory(3, 1)
 
-        def quantise_chunk(c):
-            grouped = stream.tile([P, PASSES, CHUNK, PACK], BF16, align_bytes=64, name="grouped")
-            for g in range(PASSES):
-                nc.vector.tensor_copy(
-                    out=grouped[:, g, :, :].rearrange("p (c i) t -> p c t i", i=4),
-                    in_=mem_raw[c][:, g, :, :].rearrange("p t (c i) -> p c t i", i=4),
-                )
-            codes = stream.tile([P, PASSES, CHUNK], U32, align_bytes=64, name="codes")
-            scales = stream.tile([P, PASSES, CHUNK], U8, align_bytes=64, name="scales")
-            for g in range(PASSES):
-                nc.vector.quantize_mx(
-                    out=codes[:, g, :].bitcast(FP8X4),
-                    scales=scales[:, g, :],
-                    in_=grouped[:, g, :, :].rearrange("p n t -> p (n t)"),
-                )
-            return codes, scales
+        grouped = [
+            per_chunk.tile([P, PASSES, CHUNK, PACK], BF16, align_bytes=64, name="grouped")
+            for c in range(CHUNKS)
+        ]
+        codes = [per_chunk.tile([P, PASSES, CHUNK], U32, align_bytes=64, name="codes") for c in range(CHUNKS)]
+        scales = [per_chunk.tile([P, PASSES, CHUNK], U8, align_bytes=64, name="scales") for c in range(CHUNKS)]
+
+        def regroup_columns(copy, c, g, first, last):
+            copy(
+                out=grouped[c][:, g, first:last, :].rearrange("p (c i) t -> p c t i", i=4),
+                in_=mem_raw[c][:, g, :, first:last].rearrange("p t (c i) -> p c t i", i=4),
+            )
+
+        def regroup(c, g):
+            cut = CHUNK - SCALAR_COLUMNS.get((c, g), 0)
+            if cut < CHUNK:
+                regroup_columns(nc.scalar.copy, c, g, cut, CHUNK)
+            regroup_columns(nc.vector.tensor_copy, c, g, 0, cut)
+
+        def regroup_around(c, g, between):
+            cut = CHUNK - SCALAR_COLUMNS.get((c, g), 0)
+            if cut < CHUNK:
+                regroup_columns(nc.scalar.copy, c, g, cut, CHUNK)
+            regroup_columns(nc.vector.tensor_copy, c, g, 0, CHUNK // 2)
+            between()
+            regroup_columns(nc.vector.tensor_copy, c, g, CHUNK // 2, cut)
+
+        def quantise(c, g):
+            nc.vector.quantize_mx(
+                out=codes[c][:, g, :].bitcast(FP8X4),
+                scales=scales[c][:, g, :],
+                in_=grouped[c][:, g, :, :].rearrange("p n t -> p (n t)"),
+            )
 
         w_grouped = keep.tile([P, BLOCKS, CH], BF16, align_bytes=64)
         w_codes = keep.tile([P, BLOCKS, PASSES * P], U32, align_bytes=64)
@@ -139,112 +167,208 @@ def tile_selfattention_pa_kernel(
 
         inv = keep.tile([P, BLOCKS], F32)
         shift = keep.tile([P, BLOCKS], F32)
+        eps = keep.tile([P, 1], F32)
 
-        columns = keep.tile([P, KINDS, BLOCKS], F32)
-        bias, gain, beta, mean, var = [columns[:, kind, :] for kind in range(KINDS)]
-        std = keep.tile([P, BLOCKS], F32)
+        def widen_vectors(vec_rows, tag):
+            vec_f32 = keep.tile([P, P], F32, name="vec_f32" + tag)
+            nc.scalar.copy(out=vec_f32[:], in_=vec_rows[:])
+            return vec_f32
 
-        vec_f32 = keep.tile([P, P], F32)
-
-        def widen_vectors():
-            nc.vector.tensor_copy(out=vec_f32[:], in_=vec_rows[:])
-
-        def turn_vectors():
+        def turn_vectors(vec_f32):
             bank = psum.tile([P, CHUNK], F32, name="bank")
             nc.tensor.transpose(bank[:, 0:P], vec_f32[:], identity[:])
-            nc.vector.tensor_copy(
-                out=columns[:].rearrange("p k b -> p (k b)"), in_=bank[:, 0 : KINDS * BLOCKS]
-            )
-            nc.vector.tensor_scalar_add(out=std[:], in0=var, scalar1=EPS)
-            nc.scalar.sqrt(out=std[:], in_=std[:])
-            nc.vector.tensor_sub(out=shift[:], in0=bias, in1=mean)
+            return bank
 
-        def fold_batch_norms():
-            nc.vector.reciprocal(out=inv[:], in_=std[:])
-            nc.vector.tensor_mul(out=inv[:], in0=inv[:], in1=gain)
-            nc.vector.tensor_mul(out=shift[:], in0=shift[:], in1=inv[:])
-            nc.vector.tensor_add(out=shift[:], in0=shift[:], in1=beta)
+        def take_vectors(bank, blocks, tag):
+            columns = keep.tile([P, KINDS, blocks], F32, name="columns" + tag)
+            nc.scalar.copy(out=columns[:].rearrange("p k b -> p (k b)"), in_=bank[:, 0 : KINDS * blocks])
+            std = keep.tile([P, blocks], F32, name="std" + tag)
+            nc.scalar.activation(out=std[:], in_=columns[:, KINDS - 1, :], func=SQRT, bias=eps[:])
+            return columns, std
 
-        def project(m, codes, scales):
+        def fold_steps(columns, std, first, blocks, tag):
+            bias, gain, beta, mean = [columns[:, kind, :] for kind in range(KINDS - 1)]
+            inv_part, shift_part = inv[:, first : first + blocks], shift[:, first : first + blocks]
+            rstd = keep.tile([P, blocks], F32, name="rstd" + tag)
+            offset = keep.tile([P, blocks], F32, name="offset" + tag)
+            product = keep.tile([P, blocks], F32, name="product" + tag)
+
+            def step_0():
+                nc.vector.reciprocal(out=rstd[:], in_=std[:])
+                nc.vector.tensor_sub(out=offset[:], in0=bias, in1=mean)
+
+            def step_1():
+                nc.vector.tensor_mul(out=inv_part, in0=rstd[:], in1=gain)
+
+            def step_2():
+                nc.vector.tensor_mul(out=product[:], in0=offset[:], in1=inv_part)
+
+            def step_3():
+                nc.vector.tensor_add(out=shift_part, in0=product[:], in1=beta)
+
+            return step_0, step_1, step_2, step_3
+
+        z = [per_chunk.tile([P, POOL_BLOCKS, CHUNK], F32, name="z") for c in range(CHUNKS)]
+        zq = [per_chunk.tile([P, 4, P], F32, name="zq") for c in range(CHUNKS)]
+
+        def convolve(c, m):
             bank = psum.tile([P, CHUNK], F32, name="bank")
             for g in range(PASSES):
                 nc.tensor.matmul_mx(
                     out=bank[:],
                     lhsT=w_codes[:, m, g * P : (g + 1) * P].bitcast(FP8X4),
                     lhsT_scale=w_scales[:, m, g * P : (g + 1) * P],
-                    rhs=codes[:, g, :].bitcast(FP8X4),
-                    rhs_scale=scales[:, g, :],
+                    rhs=codes[c][:, g, :].bitcast(FP8X4),
+                    rhs_scale=scales[c][:, g, :],
                     start=(g == 0),
                     stop=(g == PASSES - 1),
                 )
-            return bank
+            if m == Q_BLOCK:
+                source, target = bank[:].rearrange("p (j s) -> p s j", s=4), zq[c][:]
+            else:
+                source, target = bank[:], z[c][:, min(m, V_BLOCKS), :]
+            nc.scalar.activation(
+                out=target, in_=source,
+                func=IDENTITY, bias=shift[:, m : m + 1], scale=inv[:, m : m + 1],
+            )
 
-        def convolve_chunk(codes, scales):
-            z = stream.tile([P, POOL_BLOCKS, CHUNK], F32, name="z", bufs=3)
-            zq = stream.tile([P, 4, P], F32, name="zq")
-            for m in range(BLOCKS):
-                bank = project(m, codes, scales)
-                if m == Q_BLOCK:
-                    source, target = bank[:].rearrange("p (j s) -> p s j", s=4), zq[:]
-                else:
-                    source, target = bank[:], z[:, min(m, V_BLOCKS), :]
-                nc.scalar.activation(
-                    out=target, in_=source,
-                    func=IDENTITY, bias=shift[:, m : m + 1], scale=inv[:, m : m + 1],
-                )
-            return zq, z
-
-
-        def finish_q(c, zq):
-            q_bank = psum.tile([P, CHUNK], F32, name="bank")
+        def finish_q(c, copy):
+            bank = psum.tile([P, CHUNK], F32, name="bank")
             for s in range(4):
-                nc.tensor.transpose(q_bank[:, s * P : (s + 1) * P], zq[:, s, :], identity[:])
-            q_rows = resident.tile([P, CHUNK], F32, name="q_rows")
-            nc.scalar.copy(out=q_rows[:], in_=q_bank[:])
+                nc.tensor.transpose(bank[:, s * P : (s + 1) * P], zq[c][:, s, :], identity[:])
+            q_rows = per_chunk.tile([P, CHUNK], F32, name="q_rows")
+            copy(out=q_rows[:], in_=bank[:])
             nc.sync.dma_start(
                 out=out_0[0, c * CHUNK : (c + 1) * CHUNK, :].rearrange("(j s) ch -> j (s ch)", s=4),
                 in_=q_rows[:],
             )
 
-        def finish_kv(c, z):
-            row_pairs = z[:].rearrange("p b (a d w) -> p (b a) d w", d=2, w=WIDTH)
-            row_max = stream.tile([P, POOL_BLOCKS * CHUNK // (2 * WIDTH), WIDTH], F32, name="row_max")
-            nc.vector.tensor_max(out=row_max[:], in0=row_pairs[:, :, 0, :], in1=row_pairs[:, :, 1, :])
-            column_pairs = row_max[:].rearrange("p (b a) (x d) -> p b (a x) d", b=POOL_BLOCKS, d=2)
-            pooled = stream.tile([P, POOL_BLOCKS, POOLED], F32, name="pooled", bufs=3)
+        row_max = [
+            per_chunk.tile([P, POOL_BLOCKS, CHUNK // 2], F32, name="row_max") for c in range(CHUNKS)
+        ]
+        pooled = [per_chunk.tile([P, POOL_BLOCKS, POOLED], F32, name="pooled") for c in range(CHUNKS)]
+
+        def pool_rows(c, first, last):
+            pairs = z[c][:, first:last, :].rearrange("p b (a d w) -> p (b a) d w", d=2, w=WIDTH)
             nc.vector.tensor_max(
-                out=pooled[:], in0=column_pairs[:, :, :, 0], in1=column_pairs[:, :, :, 1]
-            )
-            nc.sync.dma_start(
-                out=out_1[0, :, c * POOLED : (c + 1) * POOLED], in_=pooled[:, V_BLOCKS, :]
+                out=row_max[c][:, first:last, :].rearrange("p b (a w) -> p (b a) w", w=WIDTH),
+                in0=pairs[:, :, 0, :], in1=pairs[:, :, 1, :],
             )
 
-            v_bank = psum.tile([P, CHUNK], F32, name="bank")
+        def pool_columns(c, first, last):
+            pairs = row_max[c][:, first:last, :].rearrange("p b (x d) -> p b x d", d=2)
+            nc.vector.tensor_max(
+                out=pooled[c][:, first:last, :], in0=pairs[:, :, :, 0], in1=pairs[:, :, :, 1]
+            )
+
+        def store_k(c):
+            nc.sync.dma_start(
+                out=out_1[0, :, c * POOLED : (c + 1) * POOLED], in_=pooled[c][:, V_BLOCKS, :]
+            )
+
+        def finish_v(c, copy):
+            bank = psum.tile([P, CHUNK], F32, name="bank")
             for b in range(V_BLOCKS):
-                nc.tensor.transpose(v_bank[:, b * P : (b + 1) * P], pooled[:, b, :], identity[:])
-            v_rows = resident.tile([P, CHUNK], F32, name="v_rows")
-            nc.scalar.copy(out=v_rows[:], in_=v_bank[:])
+                nc.tensor.transpose(bank[:, b * P : (b + 1) * P], pooled[c][:, b, :], identity[:])
+            v_rows = per_chunk.tile([P, CHUNK], F32, name="v_rows")
+            copy(out=v_rows[:], in_=bank[:])
             nc.sync.dma_start(out=out_2[0, c * POOLED : (c + 1) * POOLED, :], in_=v_rows[:])
 
-        quantised = [quantise_chunk(0)]
+        def pool(c):
+            pool_rows(c, 0, V_BLOCKS)
+            pool_rows(c, V_BLOCKS, POOL_BLOCKS)
+            pool_columns(c, 0, V_BLOCKS)
+            pool_columns(c, V_BLOCKS, POOL_BLOCKS)
+            store_k(c)
+
+        nc.vector.memset(eps[:], 0.0)
+        nc.vector.tensor_scalar_add(out=eps[:], in0=eps[:], scalar1=EPS)
+        regroup(0, 0)
+        quantise(0, 0)
         transpose_weights(0)
+        v_bank = turn_vectors(widen_vectors(v_vec_rows, "_v"))
+        fold_v = fold_steps(*take_vectors(v_bank, V_BLOCKS, "_v"), 0, V_BLOCKS, "_v")
         transpose_weights(1)
-        quantise_weights(0, 2)
-        widen_vectors()
+        regroup(0, 1)
+        quantise_weights(0, 1)
+        quantise(0, 1)
         transpose_weights(2)
+        for step in fold_v:
+            step()
+        quantise_weights(1, 1)
+        convolve(0, 0)
         transpose_weights(3)
+        convolve(0, 1)
+        regroup(1, 0)
+        regroup(1, 1)
         transpose_weights(Q_BLOCK)
-        turn_vectors()
-        quantise_weights(2, 2)
         transpose_weights(K_BLOCK)
-        fold_batch_norms()
-        quantise_weights(Q_BLOCK, 2)
-        results = []
-        for c in range(CHUNKS + 2):
-            if c < CHUNKS:
-                if c > 0:
-                    quantised.append(quantise_chunk(c))
-                results.append(convolve_chunk(*quantised[c]))
-                finish_q(c, results[c][0])
-            if c >= 2:
-                finish_kv(c - 2, results[c - 2][1])
+        quantise_weights(2, 2)
+        quantise(1, 0)
+        quantise(1, 1)
+        convolve(0, 2)
+        qk_f32 = widen_vectors(qk_vec_rows, "_qk")
+        convolve(0, 3)
+        convolve(1, 0)
+        qk_bank = turn_vectors(qk_f32)
+        fold_qk = fold_steps(*take_vectors(qk_bank, 2, "_qk"), Q_BLOCK, 2, "_qk")
+        convolve(1, 1)
+        regroup(2, 0)
+        regroup(2, 1)
+        fold_qk[0]()
+        quantise_weights(Q_BLOCK, 1)
+        fold_qk[1]()
+        quantise_weights(K_BLOCK, 1)
+        fold_qk[2]()
+        quantise(2, 0)
+        fold_qk[3]()
+        quantise(2, 1)
+        convolve(1, 2)
+        convolve(1, 3)
+        convolve(0, Q_BLOCK)
+        convolve(0, K_BLOCK)
+        pool_rows(0, 0, V_BLOCKS)
+        convolve(1, Q_BLOCK)
+        convolve(1, K_BLOCK)
+        finish_q(0, nc.scalar.copy)
+        regroup(3, 0)
+        regroup(3, 1)
+        pool_columns(0, 0, V_BLOCKS)
+        quantise(3, 0)
+        quantise(3, 1)
+        for m in range(4):
+            convolve(2, m)
+        finish_q(1, nc.scalar.copy)
+        finish_v(0, nc.scalar.copy)
+        pool_rows(1, 0, V_BLOCKS)
+        pool_rows(0, V_BLOCKS, POOL_BLOCKS)
+        pool_columns(1, 0, V_BLOCKS)
+        pool_columns(0, V_BLOCKS, POOL_BLOCKS)
+        store_k(0)
+        convolve(2, Q_BLOCK)
+        convolve(2, K_BLOCK)
+        convolve(3, 0)
+        convolve(3, 1)
+        finish_v(1, nc.vector.tensor_copy)
+        pool_rows(2, 0, V_BLOCKS)
+        finish_q(2, nc.vector.tensor_copy)
+        convolve(3, 2)
+        convolve(3, 3)
+        pool_rows(1, V_BLOCKS, POOL_BLOCKS)
+        pool_columns(2, 0, V_BLOCKS)
+        pool_columns(1, V_BLOCKS, POOL_BLOCKS)
+        store_k(1)
+        convolve(3, K_BLOCK)
+        convolve(3, Q_BLOCK)
+        finish_v(2, nc.scalar.copy)
+        finish_q(3, nc.scalar.copy)
+        pool_rows(3, 0, 2)
+        pool_rows(2, V_BLOCKS, POOL_BLOCKS)
+        pool_rows(3, 2, V_BLOCKS)
+        pool_columns(2, V_BLOCKS, POOL_BLOCKS)
+        store_k(2)
+        pool_columns(3, 0, V_BLOCKS)
+        finish_v(3, nc.scalar.copy)
+        pool_rows(3, V_BLOCKS, POOL_BLOCKS)
+        pool_columns(3, V_BLOCKS, POOL_BLOCKS)
+        store_k(3)

@@ -28,7 +28,7 @@ BLOCKS = 6
 POOL_BLOCKS = V_BLOCKS + 1
 KINDS = 5
 EPS = 1e-5
-SCALAR_COLUMNS = {(0, 0): 160}
+SCALAR_COLUMNS = {(0, 0): 160, (0, 1): 128, (1, 1): 192}
 
 FLOPS = 2 * BLOCKS * P * CH * POSITIONS
 
@@ -117,19 +117,11 @@ def tile_selfattention_pa_kernel(
                 in_=mem_raw[c][:, g, :, first:last].rearrange("p t (c i) -> p c t i", i=4),
             )
 
-        def regroup(c, g):
-            cut = CHUNK - SCALAR_COLUMNS.get((c, g), 0)
-            if cut < CHUNK:
-                regroup_columns(nc.scalar.copy, c, g, cut, CHUNK)
-            regroup_columns(nc.vector.tensor_copy, c, g, 0, cut)
+        def regroup_on_vector(c, g):
+            regroup_columns(nc.vector.tensor_copy, c, g, 0, CHUNK - SCALAR_COLUMNS.get((c, g), 0))
 
-        def regroup_around(c, g, between):
-            cut = CHUNK - SCALAR_COLUMNS.get((c, g), 0)
-            if cut < CHUNK:
-                regroup_columns(nc.scalar.copy, c, g, cut, CHUNK)
-            regroup_columns(nc.vector.tensor_copy, c, g, 0, CHUNK // 2)
-            between()
-            regroup_columns(nc.vector.tensor_copy, c, g, CHUNK // 2, cut)
+        def regroup_on_scalar(c, g):
+            regroup_columns(nc.scalar.copy, c, g, CHUNK - SCALAR_COLUMNS[c, g], CHUNK)
 
         def quantise(c, g):
             nc.vector.quantize_mx(
@@ -266,41 +258,45 @@ def tile_selfattention_pa_kernel(
                 out=out_1[0, :, c * POOLED : (c + 1) * POOLED], in_=pooled[c][:, V_BLOCKS, :]
             )
 
-        def finish_v(c, copy):
+        def finish_v(c, copy, first=0, last=V_BLOCKS):
             bank = psum.tile([P, CHUNK], F32, name="bank")
-            for b in range(V_BLOCKS):
-                nc.tensor.transpose(bank[:, b * P : (b + 1) * P], pooled[c][:, b, :], identity[:])
-            v_rows = per_chunk.tile([P, CHUNK], F32, name="v_rows")
-            copy(out=v_rows[:], in_=bank[:])
-            nc.sync.dma_start(out=out_2[0, c * POOLED : (c + 1) * POOLED, :], in_=v_rows[:])
-
-        def pool(c):
-            pool_rows(c, 0, V_BLOCKS)
-            pool_rows(c, V_BLOCKS, POOL_BLOCKS)
-            pool_columns(c, 0, V_BLOCKS)
-            pool_columns(c, V_BLOCKS, POOL_BLOCKS)
-            store_k(c)
+            v_rows = per_chunk.tile([P, CHUNK], F32, name="v_rows%d" % first)
+            width = (last - first) * P
+            for b in range(first, last):
+                nc.tensor.transpose(
+                    bank[:, (b - first) * P : (b - first + 1) * P], pooled[c][:, b, :], identity[:]
+                )
+            copy(out=v_rows[:, 0:width], in_=bank[:, 0:width])
+            nc.sync.dma_start(
+                out=out_2[0, c * POOLED : (c + 1) * POOLED, first * P : last * P], in_=v_rows[:, 0:width]
+            )
 
         nc.vector.memset(eps[:], 0.0)
         nc.vector.tensor_scalar_add(out=eps[:], in0=eps[:], scalar1=EPS)
-        regroup(0, 0)
+        regroup_on_scalar(0, 0)
+        regroup_on_vector(0, 0)
         quantise(0, 0)
         transpose_weights(0)
-        v_bank = turn_vectors(widen_vectors(v_vec_rows, "_v"))
+        v_f32 = widen_vectors(v_vec_rows, "_v")
+        v_bank = turn_vectors(v_f32)
+        regroup_on_scalar(0, 1)
         fold_v = fold_steps(*take_vectors(v_bank, V_BLOCKS, "_v"), 0, V_BLOCKS, "_v")
         transpose_weights(1)
-        regroup(0, 1)
+        regroup_on_vector(0, 1)
         quantise_weights(0, 1)
         quantise(0, 1)
         transpose_weights(2)
-        for step in fold_v:
-            step()
+        fold_v[0]()
+        fold_v[1]()
+        fold_v[2]()
         quantise_weights(1, 1)
+        fold_v[3]()
         convolve(0, 0)
         transpose_weights(3)
+        regroup_on_scalar(1, 1)
         convolve(0, 1)
-        regroup(1, 0)
-        regroup(1, 1)
+        regroup_on_vector(1, 0)
+        regroup_on_vector(1, 1)
         transpose_weights(Q_BLOCK)
         transpose_weights(K_BLOCK)
         quantise_weights(2, 2)
@@ -313,16 +309,16 @@ def tile_selfattention_pa_kernel(
         qk_bank = turn_vectors(qk_f32)
         fold_qk = fold_steps(*take_vectors(qk_bank, 2, "_qk"), Q_BLOCK, 2, "_qk")
         convolve(1, 1)
-        regroup(2, 0)
-        regroup(2, 1)
+        regroup_on_vector(2, 0)
+        regroup_on_vector(2, 1)
+        quantise(2, 0)
         fold_qk[0]()
         quantise_weights(Q_BLOCK, 1)
         fold_qk[1]()
         quantise_weights(K_BLOCK, 1)
         fold_qk[2]()
-        quantise(2, 0)
-        fold_qk[3]()
         quantise(2, 1)
+        fold_qk[3]()
         convolve(1, 2)
         convolve(1, 3)
         convolve(0, Q_BLOCK)
@@ -331,8 +327,8 @@ def tile_selfattention_pa_kernel(
         convolve(1, Q_BLOCK)
         convolve(1, K_BLOCK)
         finish_q(0, nc.scalar.copy)
-        regroup(3, 0)
-        regroup(3, 1)
+        regroup_on_vector(3, 0)
+        regroup_on_vector(3, 1)
         pool_columns(0, 0, V_BLOCKS)
         quantise(3, 0)
         quantise(3, 1)
@@ -349,8 +345,8 @@ def tile_selfattention_pa_kernel(
         convolve(2, K_BLOCK)
         convolve(3, 0)
         convolve(3, 1)
-        finish_v(1, nc.vector.tensor_copy)
         pool_rows(2, 0, V_BLOCKS)
+        finish_v(1, nc.vector.tensor_copy)
         finish_q(2, nc.vector.tensor_copy)
         convolve(3, 2)
         convolve(3, 3)
@@ -362,13 +358,14 @@ def tile_selfattention_pa_kernel(
         convolve(3, Q_BLOCK)
         finish_v(2, nc.scalar.copy)
         finish_q(3, nc.scalar.copy)
-        pool_rows(3, 0, 2)
+        pool_rows(3, 0, V_BLOCKS)
         pool_rows(2, V_BLOCKS, POOL_BLOCKS)
-        pool_rows(3, 2, V_BLOCKS)
+        pool_columns(3, 0, 2)
+        pool_columns(3, 2, V_BLOCKS)
+        pool_rows(3, V_BLOCKS, POOL_BLOCKS)
         pool_columns(2, V_BLOCKS, POOL_BLOCKS)
         store_k(2)
-        pool_columns(3, 0, V_BLOCKS)
-        finish_v(3, nc.scalar.copy)
-        pool_rows(3, V_BLOCKS, POOL_BLOCKS)
         pool_columns(3, V_BLOCKS, POOL_BLOCKS)
         store_k(3)
+        finish_v(3, nc.scalar.copy, 0, 2)
+        finish_v(3, nc.scalar.copy, 2, V_BLOCKS)

@@ -28,7 +28,7 @@ BLOCKS = 6
 POOL_BLOCKS = V_BLOCKS + 1
 KINDS = 5
 EPS = 1e-5
-SCALAR_COLUMNS = {(0, 0): 160, (0, 1): 128, (1, 1): 192}
+SCALAR_COLUMNS = {(0, 0): 160, (0, 1): 128, (1, 1): 192, (3, 0): 128}
 
 FLOPS = 2 * BLOCKS * P * CH * POSITIONS
 
@@ -321,51 +321,55 @@ def tile_selfattention_pa_kernel(
         fold_qk[3]()
         convolve(1, 2)
         convolve(1, 3)
-        convolve(0, Q_BLOCK)
-        convolve(0, K_BLOCK)
-        pool_rows(0, 0, V_BLOCKS)
-        convolve(1, Q_BLOCK)
-        convolve(1, K_BLOCK)
-        finish_q(0, nc.scalar.copy)
+        regroup_on_scalar(3, 0)
         regroup_on_vector(3, 0)
         regroup_on_vector(3, 1)
-        pool_columns(0, 0, V_BLOCKS)
+        convolve(0, Q_BLOCK)
+        convolve(1, Q_BLOCK)
         quantise(3, 0)
         quantise(3, 1)
-        for m in range(4):
-            convolve(2, m)
-        finish_q(1, nc.scalar.copy)
-        finish_v(0, nc.scalar.copy)
-        pool_rows(1, 0, V_BLOCKS)
-        pool_rows(0, V_BLOCKS, POOL_BLOCKS)
-        pool_columns(1, 0, V_BLOCKS)
-        pool_columns(0, V_BLOCKS, POOL_BLOCKS)
-        store_k(0)
+        convolve(2, 0)
+        convolve(2, 1)
+        finish_q(0, nc.scalar.copy)
+        convolve(2, 2)
+        convolve(2, 3)
         convolve(2, Q_BLOCK)
-        convolve(2, K_BLOCK)
+
+        pool_rows(0, 0, V_BLOCKS)
+        pool_rows(1, 0, V_BLOCKS)
+        pool_columns(0, 0, V_BLOCKS)
+        pool_columns(1, 0, V_BLOCKS)
+        finish_q(1, nc.scalar.copy)
+        convolve(3, Q_BLOCK)
         convolve(3, 0)
         convolve(3, 1)
-        pool_rows(2, 0, V_BLOCKS)
-        finish_v(1, nc.vector.tensor_copy)
         finish_q(2, nc.vector.tensor_copy)
+        pool_rows(2, 0, V_BLOCKS)
         convolve(3, 2)
         convolve(3, 3)
-        pool_rows(1, V_BLOCKS, POOL_BLOCKS)
-        pool_columns(2, 0, V_BLOCKS)
-        pool_columns(1, V_BLOCKS, POOL_BLOCKS)
-        store_k(1)
-        convolve(3, K_BLOCK)
-        convolve(3, Q_BLOCK)
-        finish_v(2, nc.scalar.copy)
         finish_q(3, nc.scalar.copy)
+        finish_v(0, nc.vector.tensor_copy)
+        pool_columns(2, 0, V_BLOCKS)
+        finish_v(1, nc.scalar.copy)
+        convolve(0, K_BLOCK)
+        convolve(1, K_BLOCK)
         pool_rows(3, 0, V_BLOCKS)
-        pool_rows(2, V_BLOCKS, POOL_BLOCKS)
+        convolve(2, K_BLOCK)
+        finish_v(2, nc.scalar.copy)
+        convolve(3, K_BLOCK)
+        pool_rows(0, V_BLOCKS, POOL_BLOCKS)
         pool_columns(3, 0, 2)
         pool_columns(3, 2, V_BLOCKS)
+        pool_rows(1, V_BLOCKS, POOL_BLOCKS)
+        pool_columns(0, V_BLOCKS, POOL_BLOCKS)
+        store_k(0)
+        pool_rows(2, V_BLOCKS, POOL_BLOCKS)
+        pool_columns(1, V_BLOCKS, POOL_BLOCKS)
+        store_k(1)
+        finish_v(3, nc.scalar.copy, 0, 2)
+        finish_v(3, nc.scalar.copy, 2, V_BLOCKS)
         pool_rows(3, V_BLOCKS, POOL_BLOCKS)
         pool_columns(2, V_BLOCKS, POOL_BLOCKS)
         store_k(2)
         pool_columns(3, V_BLOCKS, POOL_BLOCKS)
         store_k(3)
-        finish_v(3, nc.scalar.copy, 0, 2)
-        finish_v(3, nc.scalar.copy, 2, V_BLOCKS)

@@ -271,17 +271,28 @@ def tile_selfattention_pa_kernel(
                 out=out_2[0, c * POOLED : (c + 1) * POOLED, first * P : last * P], in_=v_rows[:, 0:width]
             )
 
+        zeros = keep.tile([P, CHUNK], BF16)
+        nc.vector.memset(zeros[:], 0.0)
+
+        def keep_warm(times):
+            bank = psum.tile([P, CHUNK], F32, name="bank")
+            for i in range(times):
+                nc.tensor.matmul(out=bank[:], lhsT=zeros[:, 0:P], rhs=zeros[:], start=True, stop=True)
+
         nc.vector.memset(eps[:], 0.0)
         nc.vector.tensor_scalar_add(out=eps[:], in0=eps[:], scalar1=EPS)
+        keep_warm(5)
         regroup_on_scalar(0, 0)
         regroup_on_vector(0, 0)
         quantise(0, 0)
         transpose_weights(0)
+        keep_warm(2)
         v_f32 = widen_vectors(v_vec_rows, "_v")
         v_bank = turn_vectors(v_f32)
         regroup_on_scalar(0, 1)
         fold_v = fold_steps(*take_vectors(v_bank, V_BLOCKS, "_v"), 0, V_BLOCKS, "_v")
         transpose_weights(1)
+        keep_warm(1)
         regroup_on_vector(0, 1)
         quantise_weights(0, 1)
         quantise(0, 1)
@@ -330,7 +341,6 @@ def tile_selfattention_pa_kernel(
         quantise(3, 1)
         convolve(2, 0)
         convolve(2, 1)
-        finish_q(0, nc.scalar.copy)
         convolve(2, 2)
         convolve(2, 3)
         convolve(2, Q_BLOCK)
@@ -339,14 +349,15 @@ def tile_selfattention_pa_kernel(
         pool_rows(1, 0, V_BLOCKS)
         pool_columns(0, 0, V_BLOCKS)
         pool_columns(1, 0, V_BLOCKS)
+        finish_q(0, nc.scalar.copy)
         finish_q(1, nc.scalar.copy)
         convolve(3, Q_BLOCK)
         convolve(3, 0)
         convolve(3, 1)
-        finish_q(2, nc.vector.tensor_copy)
         pool_rows(2, 0, V_BLOCKS)
         convolve(3, 2)
         convolve(3, 3)
+        finish_q(2, nc.vector.tensor_copy)
         finish_q(3, nc.scalar.copy)
         finish_v(0, nc.vector.tensor_copy)
         pool_columns(2, 0, V_BLOCKS)

from contextlib import ExitStack

import concourse.masks as masks
import concourse.mybir as mybir

F32 = mybir.dt.float32
BF16 = mybir.dt.bfloat16
U32 = mybir.dt.uint32
U8 = mybir.dt.uint8
FP8X4 = mybir.dt.float8_e4m3fn_x4
IDENTITY = mybir.ActivationFunctionType.Identity
SQRT = mybir.ActivationFunctionType.Sqrt

P = 128
PACK = 4
K_PASS = P * PACK
CH = 1024
PASSES = CH // K_PASS
WIDTH = 64
POSITIONS = 32 * WIDTH
CHUNK = 512
CHUNKS = POSITIONS // CHUNK
POOLED = CHUNK // 4
V_BLOCKS = 4
Q_BLOCK = 4
K_BLOCK = 5
BLOCKS = 6
POOL_BLOCKS = V_BLOCKS + 1
KINDS = 5
EPS = 1e-5
SCALAR_COLUMNS = {(0, 0): 160, (0, 1): 128, (1, 1): 192, (3, 0): 128}

FLOPS = 2 * BLOCKS * P * CH * POSITIONS


def tile_selfattention_pa_kernel(
    tc,
    memory,
    wq, bq, bnq_s, bnq_b, bnq_m, bnq_v,
    wk, bk, bnk_s, bnk_b, bnk_m, bnk_v,
    wv, bv, bnv_s, bnv_b, bnv_m, bnv_v,
    out_0, out_1, out_2,
):
    nc = tc.nc
    with ExitStack() as ctx:
        keep = ctx.enter_context(tc.tile_pool(name="keep", bufs=1))
        per_chunk = ctx.enter_context(tc.tile_pool(name="per_chunk", bufs=CHUNKS))
        stream = ctx.enter_context(tc.tile_pool(name="stream", bufs=2))
        psum = ctx.enter_context(tc.psum_pool(name="psum", bufs=8))
        ctx.enter_context(tc.manual_schedule())

        v_vec_rows = keep.tile([P, P], BF16)
        nc.gpsimd.memset(v_vec_rows[:], 0.0)
        qk_vec_rows = keep.tile([P, P], BF16)
        nc.gpsimd.memset(qk_vec_rows[:], 0.0)
        warm = keep.tile([P, 1], F32)
        nc.vector.memset(warm[:], 1.0)
        nc.scalar.sqrt(out=warm[:], in_=warm[:])
        identity = keep.tile([P, P], F32)
        nc.vector.memset(identity[:], 0.0)
        masks.make_identity(nc, identity[:], nomemset=True)
        q_vectors = (bq, bnq_s, bnq_b, bnq_m, bnq_v)
        k_vectors = (bk, bnk_s, bnk_b, bnk_m, bnk_v)
        v_vectors = (bv, bnv_s, bnv_b, bnv_m, bnv_v)

        def load_vectors(vec_rows, vectors, blocks, first, count):
            for kind, vector in enumerate(vectors):
                row = blocks * kind + first
                nc.sync.dma_start(
                    out=vec_rows[row : row + count, :],
                    in_=vector.rearrange("(b c) -> b c", c=P),
                )

        mem_rows = memory.rearrange("b (g p t) h w -> p (b g) t (h w)", p=P, t=PACK)
        mem_raw = [per_chunk.tile([P, PASSES, PACK, CHUNK], BF16, name="mem_raw") for c in range(CHUNKS)]

        def load_memory(c, g):
            nc.sync.dma_start(
                out=mem_raw[c][:, g, :, :], in_=mem_rows[:, g, :, c * CHUNK : (c + 1) * CHUNK]
            )

        w_raw = keep.tile([P, BLOCKS, CH], BF16)
        wv_blocks = wv.rearrange("(b r) k -> r b k", r=P)

        def load_v_weights(first, blocks):
            nc.sync.dma_start(
                out=w_raw[:, first : first + blocks, :], in_=wv_blocks[:, first : first + blocks, :]
            )

        load_memory(0, 0)
        load_v_weights(0, 1)
        load_memory(0, 1)
        load_vectors(v_vec_rows, v_vectors, V_BLOCKS, 0, V_BLOCKS)
        load_v_weights(1, 1)
        load_v_weights(2, 2)
        load_memory(1, 0)
        load_vectors(qk_vec_rows, q_vectors, 2, 0, 1)
        load_memory(1, 1)
        nc.sync.dma_start(out=w_raw[:, Q_BLOCK, :], in_=wq)
        nc.sync.dma_start(out=w_raw[:, K_BLOCK, :], in_=wk)
        load_memory(2, 0)
        load_memory(2, 1)
        load_vectors(qk_vec_rows, k_vectors, 2, 1, 1)
        load_memory(3, 0)
        load_memory(3, 1)

        grouped = [
            per_chunk.tile([P, PASSES, CHUNK, PACK], BF16, align_bytes=64, name="grouped")
            for c in range(CHUNKS)
        ]
        codes = [per_chunk.tile([P, PASSES, CHUNK], U32, align_bytes=64, name="codes") for c in range(CHUNKS)]
        scales = [per_chunk.tile([P, PASSES, CHUNK], U8, align_bytes=64, name="scales") for c in range(CHUNKS)]

        def regroup_columns(copy, c, g, first, last):
            copy(
                out=grouped[c][:, g, first:last, :].rearrange("p (c i) t -> p c t i", i=4),
                in_=mem_raw[c][:, g, :, first:last].rearrange("p t (c i) -> p c t i", i=4),
            )

        def regroup_on_vector(c, g):
            regroup_columns(nc.vector.tensor_copy, c, g, 0, CHUNK - SCALAR_COLUMNS.get((c, g), 0))

        def regroup_on_scalar(c, g):
            regroup_columns(nc.scalar.copy, c, g, CHUNK - SCALAR_COLUMNS[c, g], CHUNK)

        def quantise(c, g):
            nc.vector.quantize_mx(
                out=codes[c][:, g, :].bitcast(FP8X4),
                scales=scales[c][:, g, :],
                in_=grouped[c][:, g, :, :].rearrange("p n t -> p (n t)"),
            )

        w_grouped = keep.tile([P, BLOCKS, CH], BF16, align_bytes=64)
        w_codes = keep.tile([P, BLOCKS, PASSES * P], U32, align_bytes=64)
        w_scales = keep.tile([P, BLOCKS, PASSES * P], U8, align_bytes=64)

        def transpose_weights(m):
            words = w_raw[:, m, :].bitcast(F32)
            bank = psum.tile([P, CHUNK], F32, name="bank")
            for g in range(PASSES):
                for u in range(2):
                    j = 2 * g + u
                    nc.tensor.transpose(
                        bank[:, j * P : (j + 1) * P],
                        words[:, 2 * P * g + u : 2 * P * (g + 1) : 2],
                        identity[:],
                    )
            nc.scalar.copy(
                out=w_grouped[:, m, :].bitcast(F32).rearrange("p (g r u) -> p g r u", g=PASSES, u=2),
                in_=bank[:].rearrange("p (g u r) -> p g r u", g=PASSES, u=2),
            )

        def quantise_weights(first, blocks):
            nc.vector.quantize_mx(
                out=w_codes[:, first : first + blocks, :].rearrange("p m w -> p (m w)").bitcast(FP8X4),
                scales=w_scales[:, first : first + blocks, :].rearrange("p m w -> p (m w)"),
                in_=w_grouped[:, first : first + blocks, :].rearrange("p m k -> p (m k)"),
            )

        inv = keep.tile([P, BLOCKS], F32)
        shift = keep.tile([P, BLOCKS], F32)
        eps = keep.tile([P, 1], F32)

        def widen_vectors(vec_rows, tag):
            vec_f32 = keep.tile([P, P], F32, name="vec_f32" + tag)
            nc.scalar.copy(out=vec_f32[:], in_=vec_rows[:])
            return vec_f32

        def turn_vectors(vec_f32):
            bank = psum.tile([P, CHUNK], F32, name="bank")
            nc.tensor.transpose(bank[:, 0:P], vec_f32[:], identity[:])
            return bank

        def take_vectors(bank, blocks, tag):
            columns = keep.tile([P, KINDS, blocks], F32, name="columns" + tag)
            nc.scalar.copy(out=columns[:].rearrange("p k b -> p (k b)"), in_=bank[:, 0 : KINDS * blocks])
            std = keep.tile([P, blocks], F32, name="std" + tag)
            nc.scalar.activation(out=std[:], in_=columns[:, KINDS - 1, :], func=SQRT, bias=eps[:])
            return columns, std

        def fold_steps(columns, std, first, blocks, tag):
            bias, gain, beta, mean = [columns[:, kind, :] for kind in range(KINDS - 1)]
            inv_part, shift_part = inv[:, first : first + blocks], shift[:, first : first + blocks]
            rstd = keep.tile([P, blocks], F32, name="rstd" + tag)
            offset = keep.tile([P, blocks], F32, name="offset" + tag)
            product = keep.tile([P, blocks], F32, name="product" + tag)

            def step_0():
                nc.vector.reciprocal(out=rstd[:], in_=std[:])
                nc.vector.tensor_sub(out=offset[:], in0=bias, in1=mean)

            def step_1():
                nc.vector.tensor_mul(out=inv_part, in0=rstd[:], in1=gain)

            def step_2():
                nc.vector.tensor_mul(out=product[:], in0=offset[:], in1=inv_part)

            def step_3():
                nc.vector.tensor_add(out=shift_part, in0=product[:], in1=beta)

            return step_0, step_1, step_2, step_3

        z = [per_chunk.tile([P, POOL_BLOCKS, CHUNK], F32, name="z") for c in range(CHUNKS)]
        zq = [per_chunk.tile([P, 4, P], F32, name="zq") for c in range(CHUNKS)]

        def convolve(c, m):
            bank = psum.tile([P, CHUNK], F32, name="bank")
            for g in range(PASSES):
                nc.tensor.matmul_mx(
                    out=bank[:],
                    lhsT=w_codes[:, m, g * P : (g + 1) * P].bitcast(FP8X4),
                    lhsT_scale=w_scales[:, m, g * P : (g + 1) * P],
                    rhs=codes[c][:, g, :].bitcast(FP8X4),
                    rhs_scale=scales[c][:, g, :],
                    start=(g == 0),
                    stop=(g == PASSES - 1),
                )
            if m == Q_BLOCK:
                source, target = bank[:].rearrange("p (j s) -> p s j", s=4), zq[c][:]
            else:
                source, target = bank[:], z[c][:, min(m, V_BLOCKS), :]
            nc.scalar.activation(
                out=target, in_=source,
                func=IDENTITY, bias=shift[:, m : m + 1], scale=inv[:, m : m + 1],
            )

        def finish_q(c, copy):
            bank = psum.tile([P, CHUNK], F32, name="bank")
            for s in range(4):
                nc.tensor.transpose(bank[:, s * P : (s + 1) * P], zq[c][:, s, :], identity[:])
            q_rows = per_chunk.tile([P, CHUNK], F32, name="q_rows")
            copy(out=q_rows[:], in_=bank[:])
            nc.sync.dma_start(
                out=out_0[0, c * CHUNK : (c + 1) * CHUNK, :].rearrange("(j s) ch -> j (s ch)", s=4),
                in_=q_rows[:],
            )

        row_max = [
            per_chunk.tile([P, POOL_BLOCKS, CHUNK // 2], F32, name="row_max") for c in range(CHUNKS)
        ]
        pooled = [per_chunk.tile([P, POOL_BLOCKS, POOLED], F32, name="pooled") for c in range(CHUNKS)]

        def pool_rows(c, first, last):
            pairs = z[c][:, first:last, :].rearrange("p b (a d w) -> p (b a) d w", d=2, w=WIDTH)
            nc.vector.tensor_max(
                out=row_max[c][:, first:last, :].rearrange("p b (a w) -> p (b a) w", w=WIDTH),
                in0=pairs[:, :, 0, :], in1=pairs[:, :, 1, :],
            )

        def pool_columns(c, first, last):
            pairs = row_max[c][:, first:last, :].rearrange("p b (x d) -> p b x d", d=2)
            nc.vector.tensor_max(
                out=pooled[c][:, first:last, :], in0=pairs[:, :, :, 0], in1=pairs[:, :, :, 1]
            )

        def store_k(c):
            nc.sync.dma_start(
                out=out_1[0, :, c * POOLED : (c + 1) * POOLED], in_=pooled[c][:, V_BLOCKS, :]
            )

        def finish_v(c, copy, first=0, last=V_BLOCKS):
            bank = psum.tile([P, CHUNK], F32, name="bank")
            v_rows = per_chunk.tile([P, CHUNK], F32, name="v_rows%d" % first)
            width = (last - first) * P
            for b in range(first, last):
                nc.tensor.transpose(
                    bank[:, (b - first) * P : (b - first + 1) * P], pooled[c][:, b, :], identity[:]
                )
            copy(out=v_rows[:, 0:width], in_=bank[:, 0:width])
            nc.sync.dma_start(
                out=out_2[0, c * POOLED : (c + 1) * POOLED, first * P : last * P], in_=v_rows[:, 0:width]
            )

        zeros = keep.tile([P, CHUNK], BF16)
        nc.vector.memset(zeros[:], 0.0)

        def keep_warm(times):
            bank = psum.tile([P, CHUNK], F32, name="bank")
            for i in range(times):
                nc.tensor.matmul(out=bank[:], lhsT=zeros[:, 0:P], rhs=zeros[:], start=True, stop=True)

        nc.vector.memset(eps[:], 0.0)
        nc.vector.tensor_scalar_add(out=eps[:], in0=eps[:], scalar1=EPS)
        keep_warm(5)
        regroup_on_scalar(0, 0)
        regroup_on_vector(0, 0)
        quantise(0, 0)
        transpose_weights(0)
        keep_warm(2)
        v_f32 = widen_vectors(v_vec_rows, "_v")
        v_bank = turn_vectors(v_f32)
        regroup_on_scalar(0, 1)
        fold_v = fold_steps(*take_vectors(v_bank, V_BLOCKS, "_v"), 0, V_BLOCKS, "_v")
        transpose_weights(1)
        keep_warm(1)
        regroup_on_vector(0, 1)
        quantise_weights(0, 1)
        quantise(0, 1)
        transpose_weights(2)
        fold_v[0]()
        fold_v[1]()
        fold_v[2]()
        quantise_weights(1, 1)
        fold_v[3]()
        convolve(0, 0)
        transpose_weights(3)
        regroup_on_scalar(1, 1)
        convolve(0, 1)
        regroup_on_vector(1, 0)
        regroup_on_vector(1, 1)
        transpose_weights(Q_BLOCK)
        transpose_weights(K_BLOCK)
        quantise_weights(2, 2)
        quantise(1, 0)
        quantise(1, 1)
        convolve(0, 2)
        qk_f32 = widen_vectors(qk_vec_rows, "_qk")
        convolve(0, 3)
        convolve(1, 0)
        qk_bank = turn_vectors(qk_f32)
        fold_qk = fold_steps(*take_vectors(qk_bank, 2, "_qk"), Q_BLOCK, 2, "_qk")
        convolve(1, 1)
        regroup_on_vector(2, 0)
        regroup_on_vector(2, 1)
        quantise(2, 0)
        fold_qk[0]()
        quantise_weights(Q_BLOCK, 1)
        fold_qk[1]()
        quantise_weights(K_BLOCK, 1)
        fold_qk[2]()
        quantise(2, 1)
        fold_qk[3]()
        convolve(1, 2)
        convolve(1, 3)
        regroup_on_scalar(3, 0)
        regroup_on_vector(3, 0)
        regroup_on_vector(3, 1)
        convolve(0, Q_BLOCK)
        convolve(1, Q_BLOCK)
        quantise(3, 0)
        quantise(3, 1)
        convolve(2, 0)
        convolve(2, 1)
        convolve(2, 2)
        convolve(2, 3)
        convolve(2, Q_BLOCK)

        pool_rows(0, 0, V_BLOCKS)
        pool_rows(1, 0, V_BLOCKS)
        pool_columns(0, 0, V_BLOCKS)
        pool_columns(1, 0, V_BLOCKS)
        finish_q(0, nc.scalar.copy)
        finish_q(1, nc.scalar.copy)
        convolve(3, Q_BLOCK)
        convolve(3, 0)
        convolve(3, 1)
        pool_rows(2, 0, V_BLOCKS)
        convolve(3, 2)
        convolve(3, 3)
        finish_q(2, nc.vector.tensor_copy)
        finish_q(3, nc.scalar.copy)
        finish_v(0, nc.vector.tensor_copy)
        pool_columns(2, 0, V_BLOCKS)
        finish_v(1, nc.scalar.copy)
        convolve(0, K_BLOCK)
        convolve(1, K_BLOCK)
        pool_rows(3, 0, V_BLOCKS)
        convolve(2, K_BLOCK)
        finish_v(2, nc.scalar.copy)
        convolve(3, K_BLOCK)
        pool_rows(0, V_BLOCKS, POOL_BLOCKS)
        pool_columns(3, 0, 2)
        pool_columns(3, 2, V_BLOCKS)
        pool_rows(1, V_BLOCKS, POOL_BLOCKS)
        pool_columns(0, V_BLOCKS, POOL_BLOCKS)
        store_k(0)
        pool_rows(2, V_BLOCKS, POOL_BLOCKS)
        pool_columns(1, V_BLOCKS, POOL_BLOCKS)
        store_k(1)
        finish_v(3, nc.scalar.copy, 0, 2)
        finish_v(3, nc.scalar.copy, 2, V_BLOCKS)
        pool_rows(3, V_BLOCKS, POOL_BLOCKS)
        pool_columns(2, V_BLOCKS, POOL_BLOCKS)
        store_k(2)
        pool_columns(3, V_BLOCKS, POOL_BLOCKS)
        store_k(3)
